import numpy as np
import ml_dtypes


def mxq(x, axis, fmt="e4m3"):
    dtype, down = {"e4m3": (ml_dtypes.float8_e4m3fn, 7), "e5m2": (ml_dtypes.float8_e5m2, 14)}[fmt]
    v = np.moveaxis(np.asarray(x, np.float32).astype(ml_dtypes.bfloat16).astype(np.float64), axis, -1)
    blocks = v.reshape(v.shape[:-1] + (-1, 32))
    amax = np.abs(blocks).max(-1, keepdims=True)
    byte = np.maximum(np.where(amax > 0, np.frexp(amax)[1] - 1 + 127, 0) - down, 1)
    scale = np.exp2(byte - 127.0)
    codes = (blocks / scale).astype(np.float32).astype(dtype).astype(np.float64)
    return np.moveaxis((codes * scale).reshape(v.shape), -1, axis)


WIDE = False


def mx_kscale(k):
    if not WIDE:
        return np.ones(k)
    levels = np.array([30, -30])
    if k % 512:
        return np.exp2(np.random.permutation(np.resize(levels, k // 32))).repeat(32)
    a = np.empty((k // 512, 16))
    for p in range(k // 512):
        a[p, :8] = np.random.permutation(np.resize(levels, 8))
        for g in range(8):
            far = levels[np.abs(levels - a[p, g]) >= 10]
            a[p, g + 8] = far[np.random.randint(len(far))]
    return np.exp2(a.ravel()).repeat(32)


BF16 = ml_dtypes.bfloat16


def bf(x):
    return np.asarray(x, np.float32).astype(BF16)


def f64(x):
    return np.asarray(x).astype(np.float64)


B, IDIM, HDIM, ODIM, S, DEPTH, NACT, NTOP = 1024, 512, 1024, 512, 128, 32, 3, 2


def sigmoid(v):
    return 1.0 / (1.0 + np.exp(-v))


def setup_inputs():
    s, t = mx_kscale(IDIM), mx_kscale(HDIM)
    return {"x": bf(np.random.standard_normal((B, IDIM)) * s),
            "hidden": bf(np.random.standard_normal((B, HDIM)) * t),
            "stack_top": bf(np.random.standard_normal((B, NTOP, S))),
            "Wi": bf(np.random.standard_normal((HDIM, IDIM)) * 0.7 / np.sqrt(IDIM) / s),
            "bi": bf(np.random.standard_normal(HDIM) * 0.2),
            "Wh": bf(np.random.standard_normal((HDIM, HDIM)) * 0.7 / np.sqrt(HDIM) / t),
            "bh": bf(np.random.standard_normal(HDIM) * 0.2),
            "W0": bf(np.random.standard_normal((HDIM, S)) * 0.5 / np.sqrt(S)),
            "b0": bf(np.random.standard_normal(HDIM) * 0.2),
            "W1": bf(np.random.standard_normal((HDIM, S)) * 0.5 / np.sqrt(S)),
            "b1": bf(np.random.standard_normal(HDIM) * 0.2)}


def reference(x, hidden, stack_top, Wi, bi, Wh, bh, W0, b0, W1, b1):
    pre = ((mxq(f64(x), 1, "e5m2") @ mxq(f64(Wi), 1, "e5m2").T) + f64(bi)
           + (mxq(f64(hidden), 1, "e5m2") @ mxq(f64(Wh), 1, "e5m2").T) + f64(bh)
           + f64(stack_top)[:, 0] @ f64(W0).T + f64(b0)
           + f64(stack_top)[:, 1] @ f64(W1).T + f64(b1))
    return sigmoid(pre)

@@ -1,0 +1,186 @@
+from contextlib import ExitStack
+
+import concourse.mybir as mybir
+from concourse.masks import make_identity
+
+B, IDIM, HDIM, S = 1024, 512, 1024, 128
+FLOPS = 2 * B * HDIM * (IDIM + HDIM + 2 * S)
+
+F32 = mybir.dt.float32
+BF16 = mybir.dt.bfloat16
+U32 = mybir.dt.uint32
+U8 = mybir.dt.uint8
+E5X4 = mybir.dt.float8_e5m2_x4
+ADD = mybir.AluOpType.add
+SIGMOID = mybir.ActivationFunctionType.Sigmoid
+
+P = 128
+WARM = 4
+
+
+def tile_stackrnn_pa_kernel(tc, x, hidden, stack_top, Wi, bi, Wh, bh, W0, b0, W1, b1, out):
+    nc = tc.nc
+    with ExitStack() as ctx:
+        const = ctx.enter_context(tc.tile_pool(name="const", bufs=1))
+        raw = ctx.enter_context(tc.tile_pool(name="raw", bufs=1))
+        keep = ctx.enter_context(tc.tile_pool(name="keep", bufs=1))
+        grp_pool = ctx.enter_context(tc.tile_pool(name="grpp", bufs=4))
+        sum_pool = ctx.enter_context(tc.tile_pool(name="sump", bufs=3))
+        o_pool = ctx.enter_context(tc.tile_pool(name="outp", bufs=4))
+        psum = ctx.enter_context(tc.psum_pool(name="psum", bufs=8))
+        ctx.enter_context(tc.manual_schedule())
+
+        bias4 = const.tile([P, HDIM], BF16, name="bias4")
+        nc.vector.memset(bias4[:], 0.0)
+        ones = const.tile([P, 512], BF16, name="ones")
+        nc.vector.memset(ones[:], 1.0)
+        act_in = const.tile([P, 8], F32, name="act_in")
+        nc.vector.memset(act_in[:], 0.0)
+        act_out = const.tile([P, 8], F32, name="act_out")
+        nc.scalar.activation(out=act_out[:], in_=act_in[:], func=SIGMOID)
+        ident_b = const.tile([P, P], BF16, name="ident_b")
+        make_identity(nc, ident_b[:])
+        ident_f = const.tile([P, P], F32, name="ident_f")
+        make_identity(nc, ident_f[:])
+
+        w_raw = []
+        for j, w in enumerate((W0, W1)):
+            t = raw.tile([P, 2, 512], BF16, name="w%draw" % j)
+            nc.sync.dma_start(out=t[:], in_=w.rearrange("(n q a) s -> q n (a s)", n=2, a=4))
+            w_raw.append(t)
+        st_view = stack_top.rearrange("(p a) j s -> p a (j s)", a=8)
+        st_raw = []
+        for i in range(2):
+            t = raw.tile([P, 4, 256], BF16, name="st%draw" % i)
+            nc.sync.dma_start(out=t[:], in_=st_view[:, 4 * i:4 * i + 4, :])
+            st_raw.append(t)
+        for i, b in enumerate((bi, bh, b0, b1)):
+            nc.sync.dma_start(out=bias4[i:i + 1, :], in_=b.rearrange("(o h) -> o h", o=1))
+        wi_raw, wh_raw, x_raw, h_raw = [], [], [], []
+        for j in range(4):
+            t = raw.tile([P, 2, IDIM], BF16, name="wi%d" % j)
+            nc.sync.dma_start(out=t[:], in_=Wi[256 * j:256 * (j + 1), :].rearrange("(q a) k -> q a k", a=2))
+            wi_raw.append(t)
+        for j in range(4):
+            t = raw.tile([P, 2, HDIM], BF16, name="wh%d" % j)
+            nc.sync.dma_start(out=t[:], in_=Wh[256 * j:256 * (j + 1), :].rearrange("(q a) k -> q a k", a=2))
+            wh_raw.append(t)
+        x_view = x.rearrange("(p a) k -> p a k", a=8)
+        h_view = hidden.rearrange("(p a) k -> p a k", a=8)
+        for c in range(4):
+            t = raw.tile([P, 2, IDIM], BF16, name="x%d" % c)
+            nc.sync.dma_start(out=t[:], in_=x_view[:, 2 * c:2 * c + 2, :])
+            x_raw.append(t)
+            t = raw.tile([P, 2, HDIM], BF16, name="h%d" % c)
+            nc.sync.dma_start(out=t[:], in_=h_view[:, 2 * c:2 * c + 2, :])
+            h_raw.append(t)
+        out_view = out.rearrange("(p a) h -> p a h", a=8)
+
+        a_codes = keep.tile([P, 3, B], U32, name="a_codes", align_bytes=64)
+        a_scales = keep.tile([P, 3, B], U8, name="a_scales", align_bytes=64)
+        w_codes = keep.tile([P, 3, HDIM], U32, name="w_codes", align_bytes=64)
+        w_scales = keep.tile([P, 3, HDIM], U8, name="w_scales", align_bytes=64)
+        wT = keep.tile([P, 2, HDIM], BF16, name="wT")
+        stT = keep.tile([P, 4, 4, P], BF16, name="stT")
+        bias_bc = keep.tile([P, HDIM], F32, name="bias_bc")
+        pb = keep.tile([P, 8, HDIM], F32, name="pb")
+
+        def copy_on(eng, dst, src):
+            if eng == "v":
+                nc.vector.tensor_copy(out=dst, in_=src)
+            else:
+                nc.scalar.copy(out=dst, in_=src)
+
+        def w_bank(j, n, eng):
+            bank = psum.tile([P, 4, P], BF16, tag="bank", name="wbank")
+            for a in range(4):
+                nc.tensor.transpose(bank[:, a, :], w_raw[j][:, n, P * a:P * (a + 1)], ident_b[:])
+            copy_on(eng, wT[:, j, 512 * n:512 * (n + 1)].rearrange("p (q a) -> p q a", a=4),
+                    bank[:].rearrange("p a q -> p q a"))
+
+        def st_bank(c, eng):
+            bank = psum.tile([P, 4, P], BF16, tag="bank", name="sbank")
+            for r in range(2):
+                for j in range(2):
+                    nc.tensor.transpose(bank[:, 2 * r + j, :],
+                                        st_raw[c // 2][:, 2 * (c % 2) + r, P * j:P * (j + 1)], ident_b[:])
+            copy_on(eng, stT[:, c, :, :], bank[:])
+
+        def bias_bank(n, eng):
+            bank = psum.tile([P, 512], F32, tag="bank", name="bbank")
+            nc.tensor.matmul(bank[:], lhsT=ones[:, 0:P], rhs=bias4[:, 512 * n:512 * (n + 1)], start=True, stop=True)
+            copy_on(eng, bias_bc[:, 512 * n:512 * (n + 1)], bank[:])
+
+        def plain_pair(a, n):
+            cols = slice(512 * n, 512 * (n + 1))
+            bank = psum.tile([P, 512], F32, tag="bank", name="pbank")
+            for j in range(2):
+                nc.tensor.matmul(bank[:], lhsT=stT[:, a // 2, 2 * (a % 2) + j, :], rhs=wT[:, j, cols],
+                                 start=(j == 0), stop=(j == 1))
+            nc.vector.tensor_tensor(out=pb[:, a, cols], in0=bank[:], in1=bias_bc[:, cols], op=ADD)
+
+        def big_bank(src, g, is_weight, codes, scales, gi, c0):
+            words = src[:].bitcast(F32)
+            bank = psum.tile([P, 4, P], F32, tag="bank", name="tbank")
+            for r in range(2):
+                for u in range(2):
+                    nc.tensor.transpose(bank[:, 2 * r + u, :], words[:, r, 256 * g + u:256 * (g + 1):2], ident_f[:])
+            grp = grp_pool.tile([P, 1024], BF16, tag="grp", name="grp", align_bytes=64)
+            gw = grp[:].bitcast(F32)
+            if is_weight:
+                nc.scalar.copy(out=gw.rearrange("p (q s) -> p q s", s=4), in_=bank[:].rearrange("p s q -> p q s"))
+            else:
+                nc.scalar.copy(out=gw.rearrange("p (r q u) -> p r q u", r=2, u=2),
+                               in_=bank[:].rearrange("p (r u) q -> p r q u", u=2))
+            nc.vector.quantize_mx(out=codes[:, gi, c0:c0 + 256].bitcast(E5X4), scales=scales[:, gi, c0:c0 + 256],
+                                  in_=grp[:])
+
+        def mx_tile(a, n):
+            rows = slice(P * a, P * (a + 1))
+            cols = slice(512 * n, 512 * (n + 1))
+            acc = psum.tile([P, 512], F32, tag="bank", name="acc")
+            for g in range(3):
+                nc.tensor.matmul_mx(out=acc[:], lhsT=a_codes[:, g, rows].bitcast(E5X4), lhsT_scale=a_scales[:, g, rows],
+                                    rhs=w_codes[:, g, cols].bitcast(E5X4), rhs_scale=w_scales[:, g, cols],
+                                    start=(g == 0), stop=(g == 2))
+            pre = sum_pool.tile([P, 512], F32, tag="pre", name="pre")
+            nc.vector.tensor_tensor(out=pre[:], in0=acc[:], in1=pb[:, a, cols], op=ADD)
+            res = o_pool.tile([P, 512], F32, tag="res", name="res")
+            nc.scalar.activation(out=res[:], in_=pre[:], func=SIGMOID)
+            nc.sync.dma_start(out=out_view[:, a, cols], in_=res[:])
+
+        warm = psum.tile([P, 512], F32, tag="bank", name="warm")
+        for i in range(WARM):
+            nc.tensor.matmul(warm[:], lhsT=ones[:, 0:P], rhs=ones[:], start=True, stop=True)
+        w_bank(0, 0, "v")
+        w_bank(0, 1, "s")
+        w_bank(1, 0, "v")
+        w_bank(1, 1, "s")
+        bias_bank(0, "v")
+        bias_bank(1, "s")
+        st_bank(0, "v")
+        st_bank(1, "s")
+        st_bank(2, "v")
+        st_bank(3, "s")
+
+        banks = []
+        for j in range(4):
+            banks.append((wi_raw[j], 0, True, w_codes, w_scales, 0, 256 * j))
+        for j in range(4):
+            for g in range(2):
+                banks.append((wh_raw[j], g, True, w_codes, w_scales, 1 + g, 256 * j))
+        for c in range(4):
+            banks.append((x_raw[c], 0, False, a_codes, a_scales, 0, 256 * c))
+            for g in range(2):
+                banks.append((h_raw[c], g, False, a_codes, a_scales, 1 + g, 256 * c))
+        pairs = [(a, n) for a in range(8) for n in range(2)]
+        for i in range(8):
+            plain_pair(*pairs[2 * i])
+            big_bank(*banks[3 * i])
+            plain_pair(*pairs[2 * i + 1])
+            big_bank(*banks[3 * i + 1])
+            big_bank(*banks[3 * i + 2])
+
+        for a in range(8):
+            for n in range(2):
+                mx_tile(a, n)

@@ -24,7 +24,7 @@ def tile_stackrnn_pa_kernel(tc, x, hidden, stack_top, Wi, bi, Wh, bh, W0, b0, W1
         const = ctx.enter_context(tc.tile_pool(name="const", bufs=1))
         raw = ctx.enter_context(tc.tile_pool(name="raw", bufs=1))
         keep = ctx.enter_context(tc.tile_pool(name="keep", bufs=1))
-        grp_pool = ctx.enter_context(tc.tile_pool(name="grpp", bufs=4))
+        grp_pool = ctx.enter_context(tc.tile_pool(name="grpp", bufs=6))
         sum_pool = ctx.enter_context(tc.tile_pool(name="sump", bufs=3))
         o_pool = ctx.enter_context(tc.tile_pool(name="outp", bufs=4))
         psum = ctx.enter_context(tc.psum_pool(name="psum", bufs=8))
@@ -119,21 +119,28 @@ def tile_stackrnn_pa_kernel(tc, x, hidden, stack_top, Wi, bi, Wh, bh, W0, b0, W1
                                  start=(j == 0), stop=(j == 1))
             nc.vector.tensor_tensor(out=pb[:, a, cols], in0=bank[:], in1=bias_bc[:, cols], op=ADD)
 
+        open_grp = {}
+
         def big_bank(src, g, is_weight, codes, scales, gi, c0):
+            half = (c0 // 256) % 2
+            if half == 0:
+                grp = grp_pool.tile([P, 2048], BF16, tag="grp", name="grp", align_bytes=64)
+                open_grp[(is_weight, gi)] = grp
+            grp = open_grp[(is_weight, gi)]
             words = src[:].bitcast(F32)
             bank = psum.tile([P, 4, P], F32, tag="bank", name="tbank")
             for r in range(2):
                 for u in range(2):
                     nc.tensor.transpose(bank[:, 2 * r + u, :], words[:, r, 256 * g + u:256 * (g + 1):2], ident_f[:])
-            grp = grp_pool.tile([P, 1024], BF16, tag="grp", name="grp", align_bytes=64)
-            gw = grp[:].bitcast(F32)
+            gw = grp[:, 1024 * half:1024 * (half + 1)].bitcast(F32)
             if is_weight:
                 nc.scalar.copy(out=gw.rearrange("p (q s) -> p q s", s=4), in_=bank[:].rearrange("p s q -> p q s"))
             else:
                 nc.scalar.copy(out=gw.rearrange("p (r q u) -> p r q u", r=2, u=2),
                                in_=bank[:].rearrange("p (r u) q -> p r q u", u=2))
-            nc.vector.quantize_mx(out=codes[:, gi, c0:c0 + 256].bitcast(E5X4), scales=scales[:, gi, c0:c0 + 256],
-                                  in_=grp[:])
+            if half == 1:
+                nc.vector.quantize_mx(out=codes[:, gi, c0 - 256:c0 + 256].bitcast(E5X4),
+                                      scales=scales[:, gi, c0 - 256:c0 + 256], in_=grp[:])
 
         def mx_tile(a, n):
             rows = slice(P * a, P * (a + 1))

@@ -48,14 +48,14 @@ def tile_stackrnn_pa_kernel(tc, x, hidden, stack_top, Wi, bi, Wh, bh, W0, b0, W1
             t = raw.tile([P, 2, 512], BF16, name="w%draw" % j)
             nc.sync.dma_start(out=t[:], in_=w.rearrange("(n q a) s -> q n (a s)", n=2, a=4))
             w_raw.append(t)
+        for i, b in enumerate((bi, bh, b0, b1)):
+            nc.sync.dma_start(out=bias4[i:i + 1, :], in_=b.rearrange("(o h) -> o h", o=1))
         st_view = stack_top.rearrange("(p a) j s -> p a (j s)", a=8)
         st_raw = []
         for i in range(2):
             t = raw.tile([P, 4, 256], BF16, name="st%draw" % i)
             nc.sync.dma_start(out=t[:], in_=st_view[:, 4 * i:4 * i + 4, :])
             st_raw.append(t)
-        for i, b in enumerate((bi, bh, b0, b1)):
-            nc.sync.dma_start(out=bias4[i:i + 1, :], in_=b.rearrange("(o h) -> o h", o=1))
         wi_raw, wh_raw, x_raw, h_raw = [], [], [], []
         for j in range(4):
             t = raw.tile([P, 2, IDIM], BF16, name="wi%d" % j)

from contextlib import ExitStack

import concourse.mybir as mybir
from concourse.masks import make_identity

B, IDIM, HDIM, S = 1024, 512, 1024, 128
FLOPS = 2 * B * HDIM * (IDIM + HDIM + 2 * S)

F32 = mybir.dt.float32
BF16 = mybir.dt.bfloat16
U32 = mybir.dt.uint32
U8 = mybir.dt.uint8
E5X4 = mybir.dt.float8_e5m2_x4
ADD = mybir.AluOpType.add
SIGMOID = mybir.ActivationFunctionType.Sigmoid

P = 128
WARM = 4


def tile_stackrnn_pa_kernel(tc, x, hidden, stack_top, Wi, bi, Wh, bh, W0, b0, W1, b1, out):
    nc = tc.nc
    with ExitStack() as ctx:
        const = ctx.enter_context(tc.tile_pool(name="const", bufs=1))
        raw = ctx.enter_context(tc.tile_pool(name="raw", bufs=1))
        keep = ctx.enter_context(tc.tile_pool(name="keep", bufs=1))
        grp_pool = ctx.enter_context(tc.tile_pool(name="grpp", bufs=6))
        sum_pool = ctx.enter_context(tc.tile_pool(name="sump", bufs=3))
        o_pool = ctx.enter_context(tc.tile_pool(name="outp", bufs=4))
        psum = ctx.enter_context(tc.psum_pool(name="psum", bufs=8))
        ctx.enter_context(tc.manual_schedule())

        bias4 = const.tile([P, HDIM], BF16, name="bias4")
        nc.vector.memset(bias4[:], 0.0)
        ones = const.tile([P, 512], BF16, name="ones")
        nc.vector.memset(ones[:], 1.0)
        act_in = const.tile([P, 8], F32, name="act_in")
        nc.vector.memset(act_in[:], 0.0)
        act_out = const.tile([P, 8], F32, name="act_out")
        nc.scalar.activation(out=act_out[:], in_=act_in[:], func=SIGMOID)
        ident_b = const.tile([P, P], BF16, name="ident_b")
        make_identity(nc, ident_b[:])
        ident_f = const.tile([P, P], F32, name="ident_f")
        make_identity(nc, ident_f[:])

        w_raw = []
        for j, w in enumerate((W0, W1)):
            t = raw.tile([P, 2, 512], BF16, name="w%draw" % j)
            nc.sync.dma_start(out=t[:], in_=w.rearrange("(n q a) s -> q n (a s)", n=2, a=4))
            w_raw.append(t)
        for i, b in enumerate((bi, bh, b0, b1)):
            nc.sync.dma_start(out=bias4[i:i + 1, :], in_=b.rearrange("(o h) -> o h", o=1))
        st_view = stack_top.rearrange("(p a) j s -> p a (j s)", a=8)
        st_raw = []
        for i in range(2):
            t = raw.tile([P, 4, 256], BF16, name="st%draw" % i)
            nc.sync.dma_start(out=t[:], in_=st_view[:, 4 * i:4 * i + 4, :])
            st_raw.append(t)
        wi_raw, wh_raw, x_raw, h_raw = [], [], [], []
        for j in range(4):
            t = raw.tile([P, 2, IDIM], BF16, name="wi%d" % j)
            nc.sync.dma_start(out=t[:], in_=Wi[256 * j:256 * (j + 1), :].rearrange("(q a) k -> q a k", a=2))
            wi_raw.append(t)
        for j in range(4):
            t = raw.tile([P, 2, HDIM], BF16, name="wh%d" % j)
            nc.sync.dma_start(out=t[:], in_=Wh[256 * j:256 * (j + 1), :].rearrange("(q a) k -> q a k", a=2))
            wh_raw.append(t)
        x_view = x.rearrange("(p a) k -> p a k", a=8)
        h_view = hidden.rearrange("(p a) k -> p a k", a=8)
        for c in range(4):
            t = raw.tile([P, 2, IDIM], BF16, name="x%d" % c)
            nc.sync.dma_start(out=t[:], in_=x_view[:, 2 * c:2 * c + 2, :])
            x_raw.append(t)
            t = raw.tile([P, 2, HDIM], BF16, name="h%d" % c)
            nc.sync.dma_start(out=t[:], in_=h_view[:, 2 * c:2 * c + 2, :])
            h_raw.append(t)
        out_view = out.rearrange("(p a) h -> p a h", a=8)

        a_codes = keep.tile([P, 3, B], U32, name="a_codes", align_bytes=64)
        a_scales = keep.tile([P, 3, B], U8, name="a_scales", align_bytes=64)
        w_codes = keep.tile([P, 3, HDIM], U32, name="w_codes", align_bytes=64)
        w_scales = keep.tile([P, 3, HDIM], U8, name="w_scales", align_bytes=64)
        wT = keep.tile([P, 2, HDIM], BF16, name="wT")
        stT = keep.tile([P, 4, 4, P], BF16, name="stT")
        bias_bc = keep.tile([P, HDIM], F32, name="bias_bc")
        pb = keep.tile([P, 8, HDIM], F32, name="pb")

        def copy_on(eng, dst, src):
            if eng == "v":
                nc.vector.tensor_copy(out=dst, in_=src)
            else:
                nc.scalar.copy(out=dst, in_=src)

        def w_bank(j, n, eng):
            bank = psum.tile([P, 4, P], BF16, tag="bank", name="wbank")
            for a in range(4):
                nc.tensor.transpose(bank[:, a, :], w_raw[j][:, n, P * a:P * (a + 1)], ident_b[:])
            copy_on(eng, wT[:, j, 512 * n:512 * (n + 1)].rearrange("p (q a) -> p q a", a=4),
                    bank[:].rearrange("p a q -> p q a"))

        def st_bank(c, eng):
            bank = psum.tile([P, 4, P], BF16, tag="bank", name="sbank")
            for r in range(2):
                for j in range(2):
                    nc.tensor.transpose(bank[:, 2 * r + j, :],
                                        st_raw[c // 2][:, 2 * (c % 2) + r, P * j:P * (j + 1)], ident_b[:])
            copy_on(eng, stT[:, c, :, :], bank[:])

        def bias_bank(n, eng):
            bank = psum.tile([P, 512], F32, tag="bank", name="bbank")
            nc.tensor.matmul(bank[:], lhsT=ones[:, 0:P], rhs=bias4[:, 512 * n:512 * (n + 1)], start=True, stop=True)
            copy_on(eng, bias_bc[:, 512 * n:512 * (n + 1)], bank[:])

        def plain_pair(a, n):
            cols = slice(512 * n, 512 * (n + 1))
            bank = psum.tile([P, 512], F32, tag="bank", name="pbank")
            for j in range(2):
                nc.tensor.matmul(bank[:], lhsT=stT[:, a // 2, 2 * (a % 2) + j, :], rhs=wT[:, j, cols],
                                 start=(j == 0), stop=(j == 1))
            nc.vector.tensor_tensor(out=pb[:, a, cols], in0=bank[:], in1=bias_bc[:, cols], op=ADD)

        open_grp = {}

        def big_bank(src, g, is_weight, codes, scales, gi, c0):
            half = (c0 // 256) % 2
            if half == 0:
                grp = grp_pool.tile([P, 2048], BF16, tag="grp", name="grp", align_bytes=64)
                open_grp[(is_weight, gi)] = grp
            grp = open_grp[(is_weight, gi)]
            words = src[:].bitcast(F32)
            bank = psum.tile([P, 4, P], F32, tag="bank", name="tbank")
            for r in range(2):
                for u in range(2):
                    nc.tensor.transpose(bank[:, 2 * r + u, :], words[:, r, 256 * g + u:256 * (g + 1):2], ident_f[:])
            gw = grp[:, 1024 * half:1024 * (half + 1)].bitcast(F32)
            if is_weight:
                nc.scalar.copy(out=gw.rearrange("p (q s) -> p q s", s=4), in_=bank[:].rearrange("p s q -> p q s"))
            else:
                nc.scalar.copy(out=gw.rearrange("p (r q u) -> p r q u", r=2, u=2),
                               in_=bank[:].rearrange("p (r u) q -> p r q u", u=2))
            if half == 1:
                nc.vector.quantize_mx(out=codes[:, gi, c0 - 256:c0 + 256].bitcast(E5X4),
                                      scales=scales[:, gi, c0 - 256:c0 + 256], in_=grp[:])

        def mx_tile(a, n):
            rows = slice(P * a, P * (a + 1))
            cols = slice(512 * n, 512 * (n + 1))
            acc = psum.tile([P, 512], F32, tag="bank", name="acc")
            for g in range(3):
                nc.tensor.matmul_mx(out=acc[:], lhsT=a_codes[:, g, rows].bitcast(E5X4), lhsT_scale=a_scales[:, g, rows],
                                    rhs=w_codes[:, g, cols].bitcast(E5X4), rhs_scale=w_scales[:, g, cols],
                                    start=(g == 0), stop=(g == 2))
            pre = sum_pool.tile([P, 512], F32, tag="pre", name="pre")
            nc.vector.tensor_tensor(out=pre[:], in0=acc[:], in1=pb[:, a, cols], op=ADD)
            res = o_pool.tile([P, 512], F32, tag="res", name="res")
            nc.scalar.activation(out=res[:], in_=pre[:], func=SIGMOID)
            nc.sync.dma_start(out=out_view[:, a, cols], in_=res[:])

        warm = psum.tile([P, 512], F32, tag="bank", name="warm")
        for i in range(WARM):
            nc.tensor.matmul(warm[:], lhsT=ones[:, 0:P], rhs=ones[:], start=True, stop=True)
        w_bank(0, 0, "v")
        w_bank(0, 1, "s")
        w_bank(1, 0, "v")
        w_bank(1, 1, "s")
        bias_bank(0, "v")
        bias_bank(1, "s")
        st_bank(0, "v")
        st_bank(1, "s")
        st_bank(2, "v")
        st_bank(3, "s")

        banks = []
        for j in range(4):
            banks.append((wi_raw[j], 0, True, w_codes, w_scales, 0, 256 * j))
        for j in range(4):
            for g in range(2):
                banks.append((wh_raw[j], g, True, w_codes, w_scales, 1 + g, 256 * j))
        for c in range(4):
            banks.append((x_raw[c], 0, False, a_codes, a_scales, 0, 256 * c))
            for g in range(2):
                banks.append((h_raw[c], g, False, a_codes, a_scales, 1 + g, 256 * c))
        pairs = [(a, n) for a in range(8) for n in range(2)]
        for i in range(8):
            plain_pair(*pairs[2 * i])
            big_bank(*banks[3 * i])
            plain_pair(*pairs[2 * i + 1])
            big_bank(*banks[3 * i + 1])
            big_bank(*banks[3 * i + 2])

        for a in range(8):
            for n in range(2):
                mx_tile(a, n)
